import numpy as np
import ml_dtypes


def mxq(x, axis, fmt="e4m3"):
    dtype, down = {"e4m3": (ml_dtypes.float8_e4m3fn, 7), "e5m2": (ml_dtypes.float8_e5m2, 14)}[fmt]
    v = np.moveaxis(np.asarray(x, np.float32).astype(ml_dtypes.bfloat16).astype(np.float64), axis, -1)
    blocks = v.reshape(v.shape[:-1] + (-1, 32))
    amax = np.abs(blocks).max(-1, keepdims=True)
    byte = np.maximum(np.where(amax > 0, np.frexp(amax)[1] - 1 + 127, 0) - down, 1)
    scale = np.exp2(byte - 127.0)
    codes = (blocks / scale).astype(np.float32).astype(dtype).astype(np.float64)
    return np.moveaxis((codes * scale).reshape(v.shape), -1, axis)


WIDE = False


def mx_kscale(k):
    if not WIDE:
        return np.ones(k)
    levels = np.array([10, -10, 5, -5, 0])
    a = np.random.permutation(np.resize(levels, k // 512 * 4)).reshape(k // 512, 4)
    idx = np.arange(k)
    return np.exp2(a[idx // 512, idx % 128 // 32])


BF16 = ml_dtypes.bfloat16


def bf(x):
    return np.asarray(x, np.float32).astype(BF16)


def f64(x):
    return np.asarray(x).astype(np.float64)


B, N, DIM, H, HKV, D, CACHE, WINDOW = 4, 2048, 512, 2, 1, 128, 1536, 1024
EPS = 1e-6
THETA = 10000.0
HALF = D // 2


def rms_norm(t, w):
    return t * (1.0 / np.sqrt(np.mean(t * t, axis=-1, keepdims=True) + EPS)) * w


def rope(t, cos, sin):
    t2 = t.reshape(*t.shape[:-1], HALF, 2)
    x0, x1 = t2[..., 0], t2[..., 1]
    c = cos[None, None, :, :]
    s = sin[None, None, :, :]
    r0 = x0 * c - x1 * s
    r1 = x0 * s + x1 * c
    return np.stack([r0, r1], axis=-1).reshape(t.shape)


def setup_inputs():
    s = mx_kscale(DIM)
    ang = np.arange(CACHE, CACHE + N)[:, None] * (1.0 / THETA ** (np.arange(0, D, 2) / D))[None, :]
    return {"x": bf(np.random.standard_normal((B, N, DIM)) * s),
            "freqs_cos": bf(np.cos(ang)), "freqs_sin": bf(np.sin(ang)),
            "Wq": bf(np.random.standard_normal((H * D, DIM)) / np.sqrt(DIM) / s[None, :]),
            "Wk": bf(np.random.standard_normal((HKV * D, DIM)) / np.sqrt(DIM) / s[None, :]),
            "Wv": bf(np.random.standard_normal((HKV * D, DIM)) / np.sqrt(DIM) / s[None, :]),
            "wq_norm": bf(2.0 + 0.2 * np.random.standard_normal(D)),
            "wk_norm": bf(1.0 + 0.1 * np.random.standard_normal(D))}


def reference(x, freqs_cos, freqs_sin, Wq, Wk, Wv, wq_norm, wk_norm):
    xq = mxq(f64(x), 2, "e4m3")
    q = (xq @ mxq(f64(Wq), 1, "e4m3").T).reshape(B, N, H, D).transpose(0, 2, 1, 3)
    k = (xq @ mxq(f64(Wk), 1, "e4m3").T).reshape(B, N, HKV, D).transpose(0, 2, 1, 3)
    v = (xq @ mxq(f64(Wv), 1, "e4m3").T).reshape(B, N, HKV, D).transpose(0, 2, 1, 3)
    q = rms_norm(q, f64(wq_norm))
    k = rms_norm(k, f64(wk_norm))
    q = rope(q, f64(freqs_cos), f64(freqs_sin))
    k = rope(k, f64(freqs_cos), f64(freqs_sin))
    return q, k, v

@@ -1,0 +1,268 @@
+from contextlib import ExitStack
+
+import concourse.mybir as mybir
+from concourse.masks import make_identity
+
+F32 = mybir.dt.float32
+BF16 = mybir.dt.bfloat16
+U32 = mybir.dt.uint32
+U8 = mybir.dt.uint8
+FP8X4 = mybir.dt.float8_e4m3fn_x4
+ALU = mybir.AluOpType
+ACT = mybir.ActivationFunctionType
+
+P = 128
+B, N, DIM, D = 4, 2048, 512, 128
+HALF = D // 2
+EPS = 1e-6
+N_HEADS = 4
+N_ROTATED = 3
+V_HEAD = 3
+WORDS = DIM // 2
+
+J = 8
+CHUNK = P * J
+HALVES = N // CHUNK
+N_CHUNKS = B * HALVES
+PAIRS_PER_CHUNK = J // 2
+N_PAIRS = N_CHUNKS * PAIRS_PER_CHUNK
+TILES_PER_STORE = 8
+
+FLOPS = 2 * B * N * DIM * (N_HEADS * D)
+
+
+def tile_slidingcacheattention_pa_t_kernel(
+    tc, x, freqs_cos, freqs_sin, Wq, Wk, Wv, wq_norm, wk_norm, out_0, out_1, out_2
+):
+    nc = tc.nc
+    with ExitStack() as ctx:
+        ctx.enter_context(tc.manual_schedule())
+        const = ctx.enter_context(tc.tile_pool(name="const", bufs=1))
+        x_pool = ctx.enter_context(tc.tile_pool(name="x_pool", bufs=N_CHUNKS))
+        mx_pool = ctx.enter_context(tc.tile_pool(name="mx_pool", bufs=3))
+        small = ctx.enter_context(tc.tile_pool(name="small", bufs=3))
+        parts = ctx.enter_context(tc.tile_pool(name="parts", bufs=3))
+        stores = ctx.enter_context(tc.tile_pool(name="stores", bufs=3))
+        turn_psum = ctx.enter_context(tc.psum_pool(name="turn_psum", bufs=2))
+        acc_psum = ctx.enter_context(tc.psum_pool(name="acc_psum", bufs=6))
+
+        w_rows = const.tile([P, N_HEADS * DIM], BF16)
+        nc.sync.dma_start(
+            out=w_rows[:, 0 : 2 * DIM].rearrange("p (f k) -> p f k", f=2),
+            in_=Wq.rearrange("(f p) k -> p f k", p=P),
+        )
+        nc.sync.dma_start(out=w_rows[:, 2 * DIM : 3 * DIM], in_=Wk)
+        nc.sync.dma_start(out=w_rows[:, 3 * DIM : 4 * DIM], in_=Wv)
+
+        x_words = []
+        for chunk in range(N_CHUNKS):
+            half, b = divmod(chunk, B)
+            x_rows = x_pool.tile([P, J * DIM], BF16, name="x_rows", tag="x_rows")
+            nc.sync.dma_start(
+                out=x_rows[:],
+                in_=x[b, half * CHUNK : (half + 1) * CHUNK, :].rearrange("(p j) k -> p (j k)", j=J),
+            )
+            x_words.append(x_rows[:].bitcast(F32))
+
+        cos_sin = const.tile([P, 3, HALVES * J, HALF], BF16)
+        for plane, freqs in enumerate((freqs_cos, freqs_sin, freqs_cos)):
+            nc.scalar.dma_start(
+                out=cos_sin[:, plane, :, :].rearrange("p (c j) i -> p c (j i)", c=HALVES),
+                in_=freqs.rearrange("(c p j) i -> p c (j i)", c=HALVES, p=P),
+            )
+        gain_rows = const.tile([P, 2, D], BF16)
+        nc.scalar.dma_start(out=gain_rows[:, 0, :], in_=wq_norm.partition_broadcast(P))
+        nc.scalar.dma_start(out=gain_rows[:, 1, :], in_=wk_norm.partition_broadcast(P))
+
+        ident = const.tile([P, P], F32)
+        make_identity(nc, ident[:])
+        eps = const.tile([P, 1], F32)
+        nc.vector.memset(eps[:], EPS)
+        warm = const.tile([P, 1], F32)
+        nc.scalar.activation(out=warm[:], in_=eps[:], func=ACT.Abs_reciprocal_sqrt)
+
+        def transpose_two_tiles(words, first_word):
+            bank = turn_psum.tile([P, 2, 2, P], F32, name="bank", tag="bank")
+            for t in range(2):
+                for u in range(2):
+                    start = first_word + t * WORDS + u * P
+                    nc.tensor.transpose(
+                        out=bank[:, t, u, :], in_=words[:, start : start + P], identity=ident[:]
+                    )
+            return bank
+
+        def regroup(bank, grouped):
+            nc.scalar.copy(
+                out=grouped.bitcast(F32).rearrange("p (t r u) -> p t r u", t=2, u=2),
+                in_=bank[:].rearrange("p t u r -> p t r u"),
+            )
+
+        w_grouped = const.tile([P, N_HEADS * D * 4], BF16, align_bytes=64)
+        w_codes = const.tile([P, N_HEADS * D], U32, align_bytes=64)
+        w_scales = const.tile([P, N_HEADS * D], U8, align_bytes=64)
+        w_words = w_rows[:].bitcast(F32)
+        for f2 in range(N_HEADS // 2):
+            bank = transpose_two_tiles(w_words, f2 * 2 * WORDS)
+            regroup(bank, w_grouped[:, f2 * 2 * D * 4 : (f2 + 1) * 2 * D * 4])
+        nc.vector.quantize_mx(out=w_codes[:].bitcast(FP8X4), scales=w_scales[:], in_=w_grouped[:])
+
+        gains = const.tile([P, 2, 2, HALF, 2], F32)
+        table = [
+            const.tile([P, HALVES * J, 2, D], F32, name="table_q"),
+            const.tile([P, HALVES * J, 2, D], F32, name="table_k"),
+        ]
+
+        def build_gains():
+            gain_pairs = gain_rows[:].rearrange("p k (i e) -> p k i e", e=2)
+            nc.vector.tensor_copy(
+                out=gains[:, :, 0, :, :], in_=gain_pairs[:, :, :, 0:1].to_broadcast([P, 2, HALF, 2])
+            )
+            nc.vector.tensor_scalar_mul(
+                out=gains[:, :, 1, :, 0:1], in0=gain_pairs[:, :, :, 1:2], scalar1=-1.0
+            )
+            nc.vector.tensor_copy(out=gains[:, :, 1, :, 1:2], in_=gain_pairs[:, :, :, 1:2])
+
+        def build_table(engine, half, kind, part):
+            tiles = slice(half * J, (half + 1) * J)
+            engine.tensor_tensor(
+                out=table[kind][:, tiles, part, :].rearrange("p t (i e) -> p t i e", e=2),
+                in0=cos_sin[:, part : part + 2, tiles, :].rearrange("p e t i -> p t i e"),
+                in1=gains[:, kind, part, :, :].unsqueeze(1).to_broadcast([P, J, HALF, 2]),
+                op=ALU.mult,
+            )
+
+        banks, grouped_tiles, codes, accs, rstds, part_tiles, store_tiles = {}, {}, {}, {}, {}, {}, {}
+
+        def stage_transpose(g):
+            chunk, pair = divmod(g, PAIRS_PER_CHUNK)
+            banks[g] = transpose_two_tiles(x_words[chunk], pair * 2 * WORDS)
+
+        def stage_regroup(g):
+            grouped = mx_pool.tile([P, 2 * P * 4], BF16, name="grouped", tag="grouped", align_bytes=64)
+            regroup(banks[g], grouped[:])
+            grouped_tiles[g] = grouped
+
+        def stage_quantise(g):
+            x_codes = mx_pool.tile([P, 2 * P], U32, name="x_codes", tag="x_codes", align_bytes=64)
+            x_scales = mx_pool.tile([P, 2 * P], U8, name="x_scales", tag="x_scales", align_bytes=64)
+            nc.vector.quantize_mx(
+                out=x_codes[:].bitcast(FP8X4), scales=x_scales[:], in_=grouped_tiles[g][:]
+            )
+            codes[g] = (x_codes, x_scales)
+
+        def stage_matmul(g):
+            x_codes, x_scales = codes[g]
+            accs[g] = []
+            for t in range(2):
+                acc = acc_psum.tile([P, N_HEADS * D], F32, name="acc", tag="acc")
+                nc.tensor.matmul_mx(
+                    out=acc[:],
+                    lhsT=x_codes[:, t * P : (t + 1) * P].bitcast(FP8X4),
+                    lhsT_scale=x_scales[:, t * P : (t + 1) * P],
+                    rhs=w_codes[:].bitcast(FP8X4),
+                    rhs_scale=w_scales[:],
+                    start=True,
+                    stop=True,
+                )
+                accs[g].append(acc)
+
+        def stage_norm(g):
+            first_tile = (2 * g) % TILES_PER_STORE
+            if first_tile == 0:
+                store_tiles[g // (TILES_PER_STORE // 2)] = stores.tile(
+                    [P, N_HEADS, TILES_PER_STORE, D], F32, name="staged", tag="staged"
+                )
+            staged = store_tiles[g // (TILES_PER_STORE // 2)]
+            squares = small.tile([P, 2 * N_ROTATED, D], BF16, name="squares", tag="squares")
+            sums = small.tile([P, 2 * N_ROTATED], F32, name="sums", tag="sums")
+            rstd = small.tile([P, 2 * N_ROTATED], F32, name="rstd", tag="rstd")
+            for t in range(2):
+                for h in range(N_ROTATED):
+                    col = t * N_ROTATED + h
+                    nc.scalar.activation(
+                        out=squares[:, col, :],
+                        in_=accs[g][t][:, h * D : (h + 1) * D],
+                        func=ACT.Square,
+                        accum_out=sums[:, col : col + 1],
+                    )
+            for t in range(2):
+                nc.scalar.copy(
+                    out=staged[:, V_HEAD, first_tile + t, :],
+                    in_=accs[g][t][:, V_HEAD * D : (V_HEAD + 1) * D],
+                )
+            nc.scalar.activation(
+                out=rstd[:], in_=sums[:], func=ACT.Abs_reciprocal_sqrt, scale=1.0 / D, bias=eps[:]
+            )
+            rstds[g] = rstd
+
+        def stage_products(g):
+            chunk, pair = divmod(g, PAIRS_PER_CHUNK)
+            half = chunk // B
+            even_odd = [
+                parts.tile([P, 2, N_ROTATED, D], F32, name="even_part", tag="even_part"),
+                parts.tile([P, 2, N_ROTATED, D], F32, name="odd_part", tag="odd_part"),
+            ]
+            for t in range(2):
+                table_tile = half * J + 2 * pair + t
+                for h in range(N_ROTATED):
+                    kind = 0 if h < 2 else 1
+                    col = t * N_ROTATED + h
+                    pairs = accs[g][t][:, h * D : (h + 1) * D].rearrange("p (i e) -> p i e", e=2)
+                    for part in range(2):
+                        nc.vector.scalar_tensor_tensor(
+                            out=even_odd[part][:, t, h, :].rearrange("p (i e) -> p i e", e=2),
+                            in0=pairs[:, :, part : part + 1].to_broadcast([P, HALF, 2]),
+                            scalar=rstds[g][:, col : col + 1],
+                            in1=table[kind][:, table_tile, part, :].rearrange("p (i e) -> p i e", e=2),
+                            op0=ALU.mult,
+                            op1=ALU.mult,
+                        )
+            part_tiles[g] = even_odd
+
+        def stage_sum(g):
+            chunk, pair = divmod(g, PAIRS_PER_CHUNK)
+            if pair == 0 and chunk < 4:
+                build_table(nc.gpsimd, 1, chunk // 2, chunk % 2)
+            first_tile = (2 * g) % TILES_PER_STORE
+            staged = store_tiles[g // (TILES_PER_STORE // 2)]
+            nc.gpsimd.tensor_tensor(
+                out=staged[:, 0:N_ROTATED, first_tile : first_tile + 2, :].rearrange("p h t d -> p t h d"),
+                in0=part_tiles[g][0][:],
+                in1=part_tiles[g][1][:],
+                op=ALU.add,
+            )
+            if first_tile + 2 == TILES_PER_STORE:
+                half, b = divmod(chunk, B)
+                tokens = slice(half * CHUNK, (half + 1) * CHUNK)
+                last = 2 * pair + 2
+                tiles = slice(last - TILES_PER_STORE, last)
+                nc.sync.dma_start(
+                    out=out_0[b, :, tokens, :].rearrange("h (p j) d -> p h j d", j=J)[:, :, tiles, :],
+                    in_=staged[:, 0:2, :, :],
+                )
+                nc.sync.dma_start(
+                    out=out_1[b, 0, tokens, :].rearrange("(p j) d -> p j d", j=J)[:, tiles, :],
+                    in_=staged[:, 2, :, :],
+                )
+                nc.sync.dma_start(
+                    out=out_2[b, 0, tokens, :].rearrange("(p j) d -> p j d", j=J)[:, tiles, :],
+                    in_=staged[:, V_HEAD, :, :],
+                )
+
+        def run(stage, g):
+            if 0 <= g < N_PAIRS:
+                stage(g)
+
+        for step in range(-4, N_PAIRS + 2):
+            run(stage_transpose, step + 4)
+            run(stage_matmul, step + 1)
+            run(stage_regroup, step + 3)
+            run(stage_norm, step)
+            run(stage_quantise, step + 2)
+            if step == -2:
+                build_gains()
+                for part in range(2):
+                    build_table(nc.vector, 0, 0, part)
+                    build_table(nc.gpsimd, 0, 1, part)
+            run(stage_products, step - 1)
+            run(stage_sum, step - 2)

@@ -19,16 +19,26 @@ N_HEADS = 4
 N_ROTATED = 3
 V_HEAD = 3
 WORDS = DIM // 2
+PACK = 4
 
 J = 8
 CHUNK = P * J
 HALVES = N // CHUNK
-N_CHUNKS = B * HALVES
-PAIRS_PER_CHUNK = J // 2
-N_PAIRS = N_CHUNKS * PAIRS_PER_CHUNK
-TILES_PER_STORE = 8
+POSITION_TILES = HALVES * J
+GROUP = 4
+PAIRS_PER_GROUP = GROUP // 2
+GROUPS_PER_CHUNK = J // GROUP
+N_GROUPS = B * HALVES * GROUPS_PER_CHUNK
+N_PAIRS = N_GROUPS * PAIRS_PER_GROUP
+N_TABLE_PIECES = (POSITION_TILES // GROUP) * 2 * 2
 
 FLOPS = 2 * B * N * DIM * (N_HEADS * D)
+
+
+def place_of_group(group):
+    chunk, part_of_chunk = divmod(group, GROUPS_PER_CHUNK)
+    half, b = divmod(chunk, B)
+    return b, half, part_of_chunk * GROUP
 
 
 def tile_slidingcacheattention_pa_t_kernel(
@@ -38,11 +48,11 @@ def tile_slidingcacheattention_pa_t_kernel(
     with ExitStack() as ctx:
         ctx.enter_context(tc.manual_schedule())
         const = ctx.enter_context(tc.tile_pool(name="const", bufs=1))
-        x_pool = ctx.enter_context(tc.tile_pool(name="x_pool", bufs=N_CHUNKS))
-        mx_pool = ctx.enter_context(tc.tile_pool(name="mx_pool", bufs=3))
+        x_pool = ctx.enter_context(tc.tile_pool(name="x_pool", bufs=N_GROUPS))
+        mx_pool = ctx.enter_context(tc.tile_pool(name="mx_pool", bufs=2))
         small = ctx.enter_context(tc.tile_pool(name="small", bufs=3))
         parts = ctx.enter_context(tc.tile_pool(name="parts", bufs=3))
-        stores = ctx.enter_context(tc.tile_pool(name="stores", bufs=3))
+        stores = ctx.enter_context(tc.tile_pool(name="stores", bufs=4))
         turn_psum = ctx.enter_context(tc.psum_pool(name="turn_psum", bufs=2))
         acc_psum = ctx.enter_context(tc.psum_pool(name="acc_psum", bufs=6))
 
@@ -55,16 +65,18 @@ def tile_slidingcacheattention_pa_t_kernel(
         nc.sync.dma_start(out=w_rows[:, 3 * DIM : 4 * DIM], in_=Wv)
 
         x_words = []
-        for chunk in range(N_CHUNKS):
-            half, b = divmod(chunk, B)
-            x_rows = x_pool.tile([P, J * DIM], BF16, name="x_rows", tag="x_rows")
+        for group in range(N_GROUPS):
+            b, half, first_tile = place_of_group(group)
+            x_rows = x_pool.tile([P, GROUP * DIM], BF16, name="x_rows", tag="x_rows")
             nc.sync.dma_start(
-                out=x_rows[:],
-                in_=x[b, half * CHUNK : (half + 1) * CHUNK, :].rearrange("(p j) k -> p (j k)", j=J),
+                out=x_rows[:].rearrange("p (j k) -> p j k", j=GROUP),
+                in_=x[b, half * CHUNK : (half + 1) * CHUNK, :].rearrange("(p j) k -> p j k", j=J)[
+                    :, first_tile : first_tile + GROUP, :
+                ],
             )
             x_words.append(x_rows[:].bitcast(F32))
 
-        cos_sin = const.tile([P, 3, HALVES * J, HALF], BF16)
+        cos_sin = const.tile([P, 3, POSITION_TILES, HALF], BF16)
         for plane, freqs in enumerate((freqs_cos, freqs_sin, freqs_cos)):
             nc.scalar.dma_start(
                 out=cos_sin[:, plane, :, :].rearrange("p (c j) i -> p c (j i)", c=HALVES),
@@ -91,74 +103,96 @@ def tile_slidingcacheattention_pa_t_kernel(
                     )
             return bank
 
-        def regroup(bank, grouped):
-            nc.scalar.copy(
-                out=grouped.bitcast(F32).rearrange("p (t r u) -> p t r u", t=2, u=2),
-                in_=bank[:].rearrange("p t u r -> p t r u"),
+        gains = const.tile([P, 2, 2, HALF, 2], F32)
+        gain_pairs = gain_rows[:].rearrange("p k (i e) -> p k i e", e=2)
+        nc.vector.tensor_copy(
+            out=gains[:, :, 0, :, :], in_=gain_pairs[:, :, :, 0:1].to_broadcast([P, 2, HALF, 2])
+        )
+        nc.vector.tensor_scalar_mul(
+            out=gains[:, :, 1, :, 0:1], in0=gain_pairs[:, :, :, 1:2], scalar1=-1.0
+        )
+        nc.vector.tensor_copy(out=gains[:, :, 1, :, 1:2], in_=gain_pairs[:, :, :, 1:2])
+
+        table = [
+            const.tile([P, POSITION_TILES, 2, D], F32, name="table_q"),
+            const.tile([P, POSITION_TILES, 2, D], F32, name="table_k"),
+        ]
+
+        def build_table_piece(piece):
+            position_group, kind_part = divmod(piece, 4)
+            kind, part = divmod(kind_part, 2)
+            tiles = slice(position_group * GROUP, (position_group + 1) * GROUP)
+            nc.vector.tensor_tensor(
+                out=table[kind][:, tiles, part, :].rearrange("p t (i e) -> p t i e", e=2),
+                in0=cos_sin[:, part : part + 2, tiles, :].rearrange("p e t i -> p t i e"),
+                in1=gains[:, kind, part, :, :].unsqueeze(1).to_broadcast([P, GROUP, HALF, 2]),
+                op=ALU.mult,
             )
 
-        w_grouped = const.tile([P, N_HEADS * D * 4], BF16, align_bytes=64)
+        for piece in range(4):
+            build_table_piece(piece)
+
+        w_grouped = const.tile([P, N_HEADS * D * PACK], BF16, align_bytes=64)
         w_codes = const.tile([P, N_HEADS * D], U32, align_bytes=64)
         w_scales = const.tile([P, N_HEADS * D], U8, align_bytes=64)
         w_words = w_rows[:].bitcast(F32)
         for f2 in range(N_HEADS // 2):
             bank = transpose_two_tiles(w_words, f2 * 2 * WORDS)
-            regroup(bank, w_grouped[:, f2 * 2 * D * 4 : (f2 + 1) * 2 * D * 4])
+            for t in range(2):
+                f = 2 * f2 + t
+                grouped_words = w_grouped[:, f * D * PACK : (f + 1) * D * PACK].bitcast(F32)
+                if f == V_HEAD:
+                    nc.scalar.copy(
+                        out=grouped_words.rearrange("p (r u) -> p r u", u=2),
+                        in_=bank[:, t, :, :].rearrange("p u r -> p r u"),
+                    )
+                else:
+                    nc.scalar.copy(
+                        out=grouped_words.rearrange("p (a i u) -> p a i u", a=2, u=2),
+                        in_=bank[:, t, :, :].rearrange("p u (i a) -> p a i u", a=2),
+                    )
         nc.vector.quantize_mx(out=w_codes[:].bitcast(FP8X4), scales=w_scales[:], in_=w_grouped[:])
-
-        gains = const.tile([P, 2, 2, HALF, 2], F32)
-        table = [
-            const.tile([P, HALVES * J, 2, D], F32, name="table_q"),
-            const.tile([P, HALVES * J, 2, D], F32, name="table_k"),
-        ]
-
-        def build_gains():
-            gain_pairs = gain_rows[:].rearrange("p k (i e) -> p k i e", e=2)
-            nc.vector.tensor_copy(
-                out=gains[:, :, 0, :, :], in_=gain_pairs[:, :, :, 0:1].to_broadcast([P, 2, HALF, 2])
-            )
-            nc.vector.tensor_scalar_mul(
-                out=gains[:, :, 1, :, 0:1], in0=gain_pairs[:, :, :, 1:2], scalar1=-1.0
-            )
-            nc.vector.tensor_copy(out=gains[:, :, 1, :, 1:2], in_=gain_pairs[:, :, :, 1:2])
-
-        def build_table(engine, half, kind, part):
-            tiles = slice(half * J, (half + 1) * J)
-            engine.tensor_tensor(
-                out=table[kind][:, tiles, part, :].rearrange("p t (i e) -> p t i e", e=2),
-                in0=cos_sin[:, part : part + 2, tiles, :].rearrange("p e t i -> p t i e"),
-                in1=gains[:, kind, part, :, :].unsqueeze(1).to_broadcast([P, J, HALF, 2]),
-                op=ALU.mult,
-            )
 
         banks, grouped_tiles, codes, accs, rstds, part_tiles, store_tiles = {}, {}, {}, {}, {}, {}, {}
 
         def stage_transpose(g):
-            chunk, pair = divmod(g, PAIRS_PER_CHUNK)
-            banks[g] = transpose_two_tiles(x_words[chunk], pair * 2 * WORDS)
+            group, pair = divmod(g, PAIRS_PER_GROUP)
+            banks[g] = transpose_two_tiles(x_words[group], pair * 2 * WORDS)
 
         def stage_regroup(g):
-            grouped = mx_pool.tile([P, 2 * P * 4], BF16, name="grouped", tag="grouped", align_bytes=64)
-            regroup(banks[g], grouped[:])
-            grouped_tiles[g] = grouped
-
-        def stage_quantise(g):
-            x_codes = mx_pool.tile([P, 2 * P], U32, name="x_codes", tag="x_codes", align_bytes=64)
-            x_scales = mx_pool.tile([P, 2 * P], U8, name="x_scales", tag="x_scales", align_bytes=64)
-            nc.vector.quantize_mx(
-                out=x_codes[:].bitcast(FP8X4), scales=x_scales[:], in_=grouped_tiles[g][:]
+            group, pair = divmod(g, PAIRS_PER_GROUP)
+            if pair == 0:
+                grouped_tiles[group] = mx_pool.tile(
+                    [P, GROUP * P * PACK], BF16, name="grouped", tag="grouped", align_bytes=64
+                )
+            columns = slice(pair * 2 * P * PACK, (pair + 1) * 2 * P * PACK)
+            nc.scalar.copy(
+                out=grouped_tiles[group][:, columns].bitcast(F32).rearrange("p (t r u) -> p t r u", t=2, u=2),
+                in_=banks[g][:].rearrange("p t u r -> p t r u"),
             )
-            codes[g] = (x_codes, x_scales)
+
+        def stage_quantise(group):
+            x_codes = mx_pool.tile([P, GROUP * P], U32, name="x_codes", tag="x_codes", align_bytes=64)
+            x_scales = mx_pool.tile([P, GROUP * P], U8, name="x_scales", tag="x_scales", align_bytes=64)
+            nc.vector.quantize_mx(
+                out=x_codes[:].bitcast(FP8X4), scales=x_scales[:], in_=grouped_tiles[group][:]
+            )
+            codes[group] = (x_codes, x_scales)
+            for piece in (4 + 2 * group, 5 + 2 * group):
+                if piece < N_TABLE_PIECES:
+                    build_table_piece(piece)
 
         def stage_matmul(g):
-            x_codes, x_scales = codes[g]
+            group, pair = divmod(g, PAIRS_PER_GROUP)
+            x_codes, x_scales = codes[group]
             accs[g] = []
             for t in range(2):
+                tokens = slice((2 * pair + t) * P, (2 * pair + t + 1) * P)
                 acc = acc_psum.tile([P, N_HEADS * D], F32, name="acc", tag="acc")
                 nc.tensor.matmul_mx(
                     out=acc[:],
-                    lhsT=x_codes[:, t * P : (t + 1) * P].bitcast(FP8X4),
-                    lhsT_scale=x_scales[:, t * P : (t + 1) * P],
+                    lhsT=x_codes[:, tokens].bitcast(FP8X4),
+                    lhsT_scale=x_scales[:, tokens],
                     rhs=w_codes[:].bitcast(FP8X4),
                     rhs_scale=w_scales[:],
                     start=True,
@@ -167,27 +201,24 @@ def tile_slidingcacheattention_pa_t_kernel(
                 accs[g].append(acc)
 
         def stage_norm(g):
-            first_tile = (2 * g) % TILES_PER_STORE
-            if first_tile == 0:
-                store_tiles[g // (TILES_PER_STORE // 2)] = stores.tile(
-                    [P, N_HEADS, TILES_PER_STORE, D], F32, name="staged", tag="staged"
-                )
-            staged = store_tiles[g // (TILES_PER_STORE // 2)]
+            group, pair = divmod(g, PAIRS_PER_GROUP)
+            if pair == 0:
+                store_tiles[group] = stores.tile([P, N_HEADS, GROUP, D], F32, name="staged", tag="staged")
             squares = small.tile([P, 2 * N_ROTATED, D], BF16, name="squares", tag="squares")
             sums = small.tile([P, 2 * N_ROTATED], F32, name="sums", tag="sums")
             rstd = small.tile([P, 2 * N_ROTATED], F32, name="rstd", tag="rstd")
             for t in range(2):
                 for h in range(N_ROTATED):
-                    col = t * N_ROTATED + h
+                    row = t * N_ROTATED + h
                     nc.scalar.activation(
-                        out=squares[:, col, :],
+                        out=squares[:, row, :],
                         in_=accs[g][t][:, h * D : (h + 1) * D],
                         func=ACT.Square,
-                        accum_out=sums[:, col : col + 1],
+                        accum_out=sums[:, row : row + 1],
                     )
             for t in range(2):
                 nc.scalar.copy(
-                    out=staged[:, V_HEAD, first_tile + t, :],
+                    out=store_tiles[group][:, V_HEAD, 2 * pair + t, :],
                     in_=accs[g][t][:, V_HEAD * D : (V_HEAD + 1) * D],
                 )
             nc.scalar.activation(
@@ -195,74 +226,72 @@ def tile_slidingcacheattention_pa_t_kernel(
             )
             rstds[g] = rstd
 
-        def stage_products(g):
-            chunk, pair = divmod(g, PAIRS_PER_CHUNK)
-            half = chunk // B
-            even_odd = [
-                parts.tile([P, 2, N_ROTATED, D], F32, name="even_part", tag="even_part"),
-                parts.tile([P, 2, N_ROTATED, D], F32, name="odd_part", tag="odd_part"),
-            ]
-            for t in range(2):
-                table_tile = half * J + 2 * pair + t
-                for h in range(N_ROTATED):
-                    kind = 0 if h < 2 else 1
-                    col = t * N_ROTATED + h
-                    pairs = accs[g][t][:, h * D : (h + 1) * D].rearrange("p (i e) -> p i e", e=2)
-                    for part in range(2):
-                        nc.vector.scalar_tensor_tensor(
-                            out=even_odd[part][:, t, h, :].rearrange("p (i e) -> p i e", e=2),
-                            in0=pairs[:, :, part : part + 1].to_broadcast([P, HALF, 2]),
-                            scalar=rstds[g][:, col : col + 1],
-                            in1=table[kind][:, table_tile, part, :].rearrange("p (i e) -> p i e", e=2),
-                            op0=ALU.mult,
-                            op1=ALU.mult,
-                        )
-            part_tiles[g] = even_odd
+        def product(g, row):
+            group, pair = divmod(g, PAIRS_PER_GROUP)
+            if pair == 0 and row == 0:
+                part_tiles[group] = parts.tile(
+                    [P, GROUP, N_ROTATED, 2, D], F32, name="even_odd", tag="even_odd"
+                )
+            t, h = divmod(row, N_ROTATED)
+            b, half, first_tile = place_of_group(group)
+            tile_in_group = 2 * pair + t
+            position_tile = half * J + first_tile + tile_in_group
+            kind = 0 if h < 2 else 1
+            nc.vector.scalar_tensor_tensor(
+                out=part_tiles[group][:, tile_in_group, h, :, :].rearrange("p a (i e) -> p (a i) e", e=2),
+                in0=accs[g][t][:, h * D : (h + 1) * D].unsqueeze(2).to_broadcast([P, D, 2]),
+                scalar=rstds[g][:, row : row + 1],
+                in1=table[kind][:, position_tile, :, :].rearrange("p a (i e) -> p (a i) e", e=2),
+                op0=ALU.mult,
+                op1=ALU.mult,
+            )
 
-        def stage_sum(g):
-            chunk, pair = divmod(g, PAIRS_PER_CHUNK)
-            if pair == 0 and chunk < 4:
-                build_table(nc.gpsimd, 1, chunk // 2, chunk % 2)
-            first_tile = (2 * g) % TILES_PER_STORE
-            staged = store_tiles[g // (TILES_PER_STORE // 2)]
+        def stage_sum(group):
+            staged = store_tiles[group]
             nc.gpsimd.tensor_tensor(
-                out=staged[:, 0:N_ROTATED, first_tile : first_tile + 2, :].rearrange("p h t d -> p t h d"),
-                in0=part_tiles[g][0][:],
-                in1=part_tiles[g][1][:],
+                out=staged[:, 0:N_ROTATED, :, :].rearrange("p h t d -> p t h d"),
+                in0=part_tiles[group][:, :, :, 0, :],
+                in1=part_tiles[group][:, :, :, 1, :],
                 op=ALU.add,
             )
-            if first_tile + 2 == TILES_PER_STORE:
-                half, b = divmod(chunk, B)
-                tokens = slice(half * CHUNK, (half + 1) * CHUNK)
-                last = 2 * pair + 2
-                tiles = slice(last - TILES_PER_STORE, last)
-                nc.sync.dma_start(
-                    out=out_0[b, :, tokens, :].rearrange("h (p j) d -> p h j d", j=J)[:, :, tiles, :],
-                    in_=staged[:, 0:2, :, :],
-                )
-                nc.sync.dma_start(
-                    out=out_1[b, 0, tokens, :].rearrange("(p j) d -> p j d", j=J)[:, tiles, :],
-                    in_=staged[:, 2, :, :],
-                )
-                nc.sync.dma_start(
-                    out=out_2[b, 0, tokens, :].rearrange("(p j) d -> p j d", j=J)[:, tiles, :],
-                    in_=staged[:, V_HEAD, :, :],
-                )
+            b, half, first_tile = place_of_group(group)
+            tokens = slice(half * CHUNK, (half + 1) * CHUNK)
+            tiles = slice(first_tile, first_tile + GROUP)
+            nc.sync.dma_start(
+                out=out_0[b, :, tokens, :].rearrange("h (p j) d -> p h j d", j=J)[:, :, tiles, :],
+                in_=staged[:, 0:2, :, :],
+            )
+            nc.sync.dma_start(
+                out=out_1[b, 0, tokens, :].rearrange("(p j) d -> p j d", j=J)[:, tiles, :],
+                in_=staged[:, 2, :, :],
+            )
+            nc.sync.dma_start(
+                out=out_2[b, 0, tokens, :].rearrange("(p j) d -> p j d", j=J)[:, tiles, :],
+                in_=staged[:, V_HEAD, :, :],
+            )
 
-        def run(stage, g):
-            if 0 <= g < N_PAIRS:
-                stage(g)
+        def in_range(g):
+            return 0 <= g < N_PAIRS
 
-        for step in range(-4, N_PAIRS + 2):
-            run(stage_transpose, step + 4)
-            run(stage_matmul, step + 1)
-            run(stage_regroup, step + 3)
-            run(stage_norm, step)
-            run(stage_quantise, step + 2)
-            if step == -2:
-                build_gains()
-                for part in range(2):
-                    build_table(nc.vector, 0, 0, part)
-                    build_table(nc.gpsimd, 0, 1, part)
-            run(stage_products, step - 1)
-            run(stage_sum, step - 2)
+        def ends_group(g):
+            return in_range(g) and g % PAIRS_PER_GROUP == PAIRS_PER_GROUP - 1
+
+        last_row = 2 * N_ROTATED - 1
+        for step in range(-5, N_PAIRS + 3):
+            if in_range(step + 5):
+                stage_transpose(step + 5)
+            if in_range(step + 1):
+                stage_matmul(step + 1)
+            if in_range(step + 4):
+                stage_regroup(step + 4)
+            if in_range(step):
+                stage_norm(step)
+            if in_range(step - 1):
+                for row in range(last_row):
+                    product(step - 1, row)
+            if ends_group(step + 3):
+                stage_quantise((step + 3) // PAIRS_PER_GROUP)
+            if in_range(step - 1):
+                product(step - 1, last_row)
+            if ends_group(step - 2):
+                stage_sum((step - 2) // PAIRS_PER_GROUP)

@@ -178,7 +178,7 @@ def tile_slidingcacheattention_pa_t_kernel(
                 out=x_codes[:].bitcast(FP8X4), scales=x_scales[:], in_=grouped_tiles[group][:]
             )
             codes[group] = (x_codes, x_scales)
-            for piece in (4 + 2 * group, 5 + 2 * group):
+            for piece in range(4 * (group + 1), 4 * (group + 2)):
                 if piece < N_TABLE_PIECES:
                     build_table_piece(piece)
 
@@ -225,6 +225,14 @@ def tile_slidingcacheattention_pa_t_kernel(
                 out=rstd[:], in_=sums[:], func=ACT.Abs_reciprocal_sqrt, scale=1.0 / D, bias=eps[:]
             )
             rstds[g] = rstd
+            if pair == PAIRS_PER_GROUP - 1:
+                b, half, first_tile = place_of_group(group)
+                nc.sync.dma_start(
+                    out=out_2[b, 0, half * CHUNK : (half + 1) * CHUNK, :].rearrange("(p j) d -> p j d", j=J)[
+                        :, first_tile : first_tile + GROUP, :
+                    ],
+                    in_=store_tiles[group][:, V_HEAD, :, :],
+                )
 
         def product(g, row):
             group, pair = divmod(g, PAIRS_PER_GROUP)
@@ -246,28 +254,25 @@ def tile_slidingcacheattention_pa_t_kernel(
                 op1=ALU.mult,
             )
 
-        def stage_sum(group):
+        def stage_sum(group, start, count):
             staged = store_tiles[group]
+            own = slice(start, start + count)
             nc.gpsimd.tensor_tensor(
-                out=staged[:, 0:N_ROTATED, :, :].rearrange("p h t d -> p t h d"),
-                in0=part_tiles[group][:, :, :, 0, :],
-                in1=part_tiles[group][:, :, :, 1, :],
+                out=staged[:, 0:N_ROTATED, own, :].rearrange("p h t d -> p t h d"),
+                in0=part_tiles[group][:, own, :, 0, :],
+                in1=part_tiles[group][:, own, :, 1, :],
                 op=ALU.add,
             )
             b, half, first_tile = place_of_group(group)
             tokens = slice(half * CHUNK, (half + 1) * CHUNK)
-            tiles = slice(first_tile, first_tile + GROUP)
+            tiles = slice(first_tile + start, first_tile + start + count)
             nc.sync.dma_start(
                 out=out_0[b, :, tokens, :].rearrange("h (p j) d -> p h j d", j=J)[:, :, tiles, :],
-                in_=staged[:, 0:2, :, :],
+                in_=staged[:, 0:2, own, :],
             )
             nc.sync.dma_start(
                 out=out_1[b, 0, tokens, :].rearrange("(p j) d -> p j d", j=J)[:, tiles, :],
-                in_=staged[:, 2, :, :],
-            )
-            nc.sync.dma_start(
-                out=out_2[b, 0, tokens, :].rearrange("(p j) d -> p j d", j=J)[:, tiles, :],
-                in_=staged[:, V_HEAD, :, :],
+                in_=staged[:, 2, own, :],
             )
 
         def in_range(g):
@@ -278,14 +283,14 @@ def tile_slidingcacheattention_pa_t_kernel(
 
         last_row = 2 * N_ROTATED - 1
         for step in range(-5, N_PAIRS + 3):
-            if in_range(step + 5):
-                stage_transpose(step + 5)
             if in_range(step + 1):
                 stage_matmul(step + 1)
-            if in_range(step + 4):
-                stage_regroup(step + 4)
+            if in_range(step + 5):
+                stage_transpose(step + 5)
             if in_range(step):
                 stage_norm(step)
+            if in_range(step + 4):
+                stage_regroup(step + 4)
             if in_range(step - 1):
                 for row in range(last_row):
                     product(step - 1, row)
@@ -293,5 +298,9 @@ def tile_slidingcacheattention_pa_t_kernel(
                 stage_quantise((step + 3) // PAIRS_PER_GROUP)
             if in_range(step - 1):
                 product(step - 1, last_row)
-            if ends_group(step - 2):
-                stage_sum((step - 2) // PAIRS_PER_GROUP)
+            if in_range(step - 2):
+                group, pair = divmod(step - 2, PAIRS_PER_GROUP)
+                if group == N_GROUPS - 1:
+                    stage_sum(group, 2 * pair, 2)
+                elif pair == PAIRS_PER_GROUP - 1:
+                    stage_sum(group, 0, GROUP)

from contextlib import ExitStack

import concourse.mybir as mybir
from concourse.masks import make_identity

F32 = mybir.dt.float32
BF16 = mybir.dt.bfloat16
U32 = mybir.dt.uint32
U8 = mybir.dt.uint8
FP8X4 = mybir.dt.float8_e4m3fn_x4
ALU = mybir.AluOpType
ACT = mybir.ActivationFunctionType

P = 128
B, N, DIM, D = 4, 2048, 512, 128
HALF = D // 2
EPS = 1e-6
N_HEADS = 4
N_ROTATED = 3
V_HEAD = 3
WORDS = DIM // 2
PACK = 4

J = 8
CHUNK = P * J
HALVES = N // CHUNK
POSITION_TILES = HALVES * J
GROUP = 4
PAIRS_PER_GROUP = GROUP // 2
GROUPS_PER_CHUNK = J // GROUP
N_GROUPS = B * HALVES * GROUPS_PER_CHUNK
N_PAIRS = N_GROUPS * PAIRS_PER_GROUP
N_TABLE_PIECES = (POSITION_TILES // GROUP) * 2 * 2

FLOPS = 2 * B * N * DIM * (N_HEADS * D)


def place_of_group(group):
    chunk, part_of_chunk = divmod(group, GROUPS_PER_CHUNK)
    half, b = divmod(chunk, B)
    return b, half, part_of_chunk * GROUP


def tile_slidingcacheattention_pa_t_kernel(
    tc, x, freqs_cos, freqs_sin, Wq, Wk, Wv, wq_norm, wk_norm, out_0, out_1, out_2
):
    nc = tc.nc
    with ExitStack() as ctx:
        ctx.enter_context(tc.manual_schedule())
        const = ctx.enter_context(tc.tile_pool(name="const", bufs=1))
        x_pool = ctx.enter_context(tc.tile_pool(name="x_pool", bufs=N_GROUPS))
        mx_pool = ctx.enter_context(tc.tile_pool(name="mx_pool", bufs=2))
        small = ctx.enter_context(tc.tile_pool(name="small", bufs=3))
        parts = ctx.enter_context(tc.tile_pool(name="parts", bufs=3))
        stores = ctx.enter_context(tc.tile_pool(name="stores", bufs=4))
        turn_psum = ctx.enter_context(tc.psum_pool(name="turn_psum", bufs=2))
        acc_psum = ctx.enter_context(tc.psum_pool(name="acc_psum", bufs=6))

        w_rows = const.tile([P, N_HEADS * DIM], BF16)
        nc.sync.dma_start(
            out=w_rows[:, 0 : 2 * DIM].rearrange("p (f k) -> p f k", f=2),
            in_=Wq.rearrange("(f p) k -> p f k", p=P),
        )
        nc.sync.dma_start(out=w_rows[:, 2 * DIM : 3 * DIM], in_=Wk)
        nc.sync.dma_start(out=w_rows[:, 3 * DIM : 4 * DIM], in_=Wv)

        x_words = []
        for group in range(N_GROUPS):
            b, half, first_tile = place_of_group(group)
            x_rows = x_pool.tile([P, GROUP * DIM], BF16, name="x_rows", tag="x_rows")
            nc.sync.dma_start(
                out=x_rows[:].rearrange("p (j k) -> p j k", j=GROUP),
                in_=x[b, half * CHUNK : (half + 1) * CHUNK, :].rearrange("(p j) k -> p j k", j=J)[
                    :, first_tile : first_tile + GROUP, :
                ],
            )
            x_words.append(x_rows[:].bitcast(F32))

        cos_sin = const.tile([P, 3, POSITION_TILES, HALF], BF16)
        for plane, freqs in enumerate((freqs_cos, freqs_sin, freqs_cos)):
            nc.scalar.dma_start(
                out=cos_sin[:, plane, :, :].rearrange("p (c j) i -> p c (j i)", c=HALVES),
                in_=freqs.rearrange("(c p j) i -> p c (j i)", c=HALVES, p=P),
            )
        gain_rows = const.tile([P, 2, D], BF16)
        nc.scalar.dma_start(out=gain_rows[:, 0, :], in_=wq_norm.partition_broadcast(P))
        nc.scalar.dma_start(out=gain_rows[:, 1, :], in_=wk_norm.partition_broadcast(P))

        ident = const.tile([P, P], F32)
        make_identity(nc, ident[:])
        eps = const.tile([P, 1], F32)
        nc.vector.memset(eps[:], EPS)
        warm = const.tile([P, 1], F32)
        nc.scalar.activation(out=warm[:], in_=eps[:], func=ACT.Abs_reciprocal_sqrt)

        def transpose_two_tiles(words, first_word):
            bank = turn_psum.tile([P, 2, 2, P], F32, name="bank", tag="bank")
            for t in range(2):
                for u in range(2):
                    start = first_word + t * WORDS + u * P
                    nc.tensor.transpose(
                        out=bank[:, t, u, :], in_=words[:, start : start + P], identity=ident[:]
                    )
            return bank

        gains = const.tile([P, 2, 2, HALF, 2], F32)
        gain_pairs = gain_rows[:].rearrange("p k (i e) -> p k i e", e=2)
        nc.vector.tensor_copy(
            out=gains[:, :, 0, :, :], in_=gain_pairs[:, :, :, 0:1].to_broadcast([P, 2, HALF, 2])
        )
        nc.vector.tensor_scalar_mul(
            out=gains[:, :, 1, :, 0:1], in0=gain_pairs[:, :, :, 1:2], scalar1=-1.0
        )
        nc.vector.tensor_copy(out=gains[:, :, 1, :, 1:2], in_=gain_pairs[:, :, :, 1:2])

        table = [
            const.tile([P, POSITION_TILES, 2, D], F32, name="table_q"),
            const.tile([P, POSITION_TILES, 2, D], F32, name="table_k"),
        ]

        def build_table_piece(piece):
            position_group, kind_part = divmod(piece, 4)
            kind, part = divmod(kind_part, 2)
            tiles = slice(position_group * GROUP, (position_group + 1) * GROUP)
            nc.vector.tensor_tensor(
                out=table[kind][:, tiles, part, :].rearrange("p t (i e) -> p t i e", e=2),
                in0=cos_sin[:, part : part + 2, tiles, :].rearrange("p e t i -> p t i e"),
                in1=gains[:, kind, part, :, :].unsqueeze(1).to_broadcast([P, GROUP, HALF, 2]),
                op=ALU.mult,
            )

        for piece in range(4):
            build_table_piece(piece)

        w_grouped = const.tile([P, N_HEADS * D * PACK], BF16, align_bytes=64)
        w_codes = const.tile([P, N_HEADS * D], U32, align_bytes=64)
        w_scales = const.tile([P, N_HEADS * D], U8, align_bytes=64)
        w_words = w_rows[:].bitcast(F32)
        for f2 in range(N_HEADS // 2):
            bank = transpose_two_tiles(w_words, f2 * 2 * WORDS)
            for t in range(2):
                f = 2 * f2 + t
                grouped_words = w_grouped[:, f * D * PACK : (f + 1) * D * PACK].bitcast(F32)
                if f == V_HEAD:
                    nc.scalar.copy(
                        out=grouped_words.rearrange("p (r u) -> p r u", u=2),
                        in_=bank[:, t, :, :].rearrange("p u r -> p r u"),
                    )
                else:
                    nc.scalar.copy(
                        out=grouped_words.rearrange("p (a i u) -> p a i u", a=2, u=2),
                        in_=bank[:, t, :, :].rearrange("p u (i a) -> p a i u", a=2),
                    )
        nc.vector.quantize_mx(out=w_codes[:].bitcast(FP8X4), scales=w_scales[:], in_=w_grouped[:])

        banks, grouped_tiles, codes, accs, rstds, part_tiles, store_tiles = {}, {}, {}, {}, {}, {}, {}

        def stage_transpose(g):
            group, pair = divmod(g, PAIRS_PER_GROUP)
            banks[g] = transpose_two_tiles(x_words[group], pair * 2 * WORDS)

        def stage_regroup(g):
            group, pair = divmod(g, PAIRS_PER_GROUP)
            if pair == 0:
                grouped_tiles[group] = mx_pool.tile(
                    [P, GROUP * P * PACK], BF16, name="grouped", tag="grouped", align_bytes=64
                )
            columns = slice(pair * 2 * P * PACK, (pair + 1) * 2 * P * PACK)
            nc.scalar.copy(
                out=grouped_tiles[group][:, columns].bitcast(F32).rearrange("p (t r u) -> p t r u", t=2, u=2),
                in_=banks[g][:].rearrange("p t u r -> p t r u"),
            )

        def stage_quantise(group):
            x_codes = mx_pool.tile([P, GROUP * P], U32, name="x_codes", tag="x_codes", align_bytes=64)
            x_scales = mx_pool.tile([P, GROUP * P], U8, name="x_scales", tag="x_scales", align_bytes=64)
            nc.vector.quantize_mx(
                out=x_codes[:].bitcast(FP8X4), scales=x_scales[:], in_=grouped_tiles[group][:]
            )
            codes[group] = (x_codes, x_scales)
            for piece in range(4 * (group + 1), 4 * (group + 2)):
                if piece < N_TABLE_PIECES:
                    build_table_piece(piece)

        def stage_matmul(g):
            group, pair = divmod(g, PAIRS_PER_GROUP)
            x_codes, x_scales = codes[group]
            accs[g] = []
            for t in range(2):
                tokens = slice((2 * pair + t) * P, (2 * pair + t + 1) * P)
                acc = acc_psum.tile([P, N_HEADS * D], F32, name="acc", tag="acc")
                nc.tensor.matmul_mx(
                    out=acc[:],
                    lhsT=x_codes[:, tokens].bitcast(FP8X4),
                    lhsT_scale=x_scales[:, tokens],
                    rhs=w_codes[:].bitcast(FP8X4),
                    rhs_scale=w_scales[:],
                    start=True,
                    stop=True,
                )
                accs[g].append(acc)

        def stage_norm(g):
            group, pair = divmod(g, PAIRS_PER_GROUP)
            if pair == 0:
                store_tiles[group] = stores.tile([P, N_HEADS, GROUP, D], F32, name="staged", tag="staged")
            squares = small.tile([P, 2 * N_ROTATED, D], BF16, name="squares", tag="squares")
            sums = small.tile([P, 2 * N_ROTATED], F32, name="sums", tag="sums")
            rstd = small.tile([P, 2 * N_ROTATED], F32, name="rstd", tag="rstd")
            for t in range(2):
                for h in range(N_ROTATED):
                    row = t * N_ROTATED + h
                    nc.scalar.activation(
                        out=squares[:, row, :],
                        in_=accs[g][t][:, h * D : (h + 1) * D],
                        func=ACT.Square,
                        accum_out=sums[:, row : row + 1],
                    )
            for t in range(2):
                nc.scalar.copy(
                    out=store_tiles[group][:, V_HEAD, 2 * pair + t, :],
                    in_=accs[g][t][:, V_HEAD * D : (V_HEAD + 1) * D],
                )
            nc.scalar.activation(
                out=rstd[:], in_=sums[:], func=ACT.Abs_reciprocal_sqrt, scale=1.0 / D, bias=eps[:]
            )
            rstds[g] = rstd
            if pair == PAIRS_PER_GROUP - 1:
                b, half, first_tile = place_of_group(group)
                nc.sync.dma_start(
                    out=out_2[b, 0, half * CHUNK : (half + 1) * CHUNK, :].rearrange("(p j) d -> p j d", j=J)[
                        :, first_tile : first_tile + GROUP, :
                    ],
                    in_=store_tiles[group][:, V_HEAD, :, :],
                )

        def product(g, row):
            group, pair = divmod(g, PAIRS_PER_GROUP)
            if pair == 0 and row == 0:
                part_tiles[group] = parts.tile(
                    [P, GROUP, N_ROTATED, 2, D], F32, name="even_odd", tag="even_odd"
                )
            t, h = divmod(row, N_ROTATED)
            b, half, first_tile = place_of_group(group)
            tile_in_group = 2 * pair + t
            position_tile = half * J + first_tile + tile_in_group
            kind = 0 if h < 2 else 1
            nc.vector.scalar_tensor_tensor(
                out=part_tiles[group][:, tile_in_group, h, :, :].rearrange("p a (i e) -> p (a i) e", e=2),
                in0=accs[g][t][:, h * D : (h + 1) * D].unsqueeze(2).to_broadcast([P, D, 2]),
                scalar=rstds[g][:, row : row + 1],
                in1=table[kind][:, position_tile, :, :].rearrange("p a (i e) -> p (a i) e", e=2),
                op0=ALU.mult,
                op1=ALU.mult,
            )

        def stage_sum(group, start, count):
            staged = store_tiles[group]
            own = slice(start, start + count)
            nc.gpsimd.tensor_tensor(
                out=staged[:, 0:N_ROTATED, own, :].rearrange("p h t d -> p t h d"),
                in0=part_tiles[group][:, own, :, 0, :],
                in1=part_tiles[group][:, own, :, 1, :],
                op=ALU.add,
            )
            b, half, first_tile = place_of_group(group)
            tokens = slice(half * CHUNK, (half + 1) * CHUNK)
            tiles = slice(first_tile + start, first_tile + start + count)
            nc.sync.dma_start(
                out=out_0[b, :, tokens, :].rearrange("h (p j) d -> p h j d", j=J)[:, :, tiles, :],
                in_=staged[:, 0:2, own, :],
            )
            nc.sync.dma_start(
                out=out_1[b, 0, tokens, :].rearrange("(p j) d -> p j d", j=J)[:, tiles, :],
                in_=staged[:, 2, own, :],
            )

        def in_range(g):
            return 0 <= g < N_PAIRS

        def ends_group(g):
            return in_range(g) and g % PAIRS_PER_GROUP == PAIRS_PER_GROUP - 1

        last_row = 2 * N_ROTATED - 1
        for step in range(-5, N_PAIRS + 3):
            if in_range(step + 1):
                stage_matmul(step + 1)
            if in_range(step + 5):
                stage_transpose(step + 5)
            if in_range(step):
                stage_norm(step)
            if in_range(step + 4):
                stage_regroup(step + 4)
            if in_range(step - 1):
                for row in range(last_row):
                    product(step - 1, row)
            if ends_group(step + 3):
                stage_quantise((step + 3) // PAIRS_PER_GROUP)
            if in_range(step - 1):
                product(step - 1, last_row)
            if in_range(step - 2):
                group, pair = divmod(step - 2, PAIRS_PER_GROUP)
                if group == N_GROUPS - 1:
                    stage_sum(group, 2 * pair, 2)
                elif pair == PAIRS_PER_GROUP - 1:
                    stage_sum(group, 0, GROUP)
